import numpy as np
import ml_dtypes


def mxq(x, axis, fmt="e4m3"):
    dtype, down = {"e4m3": (ml_dtypes.float8_e4m3fn, 7), "e5m2": (ml_dtypes.float8_e5m2, 14)}[fmt]
    v = np.moveaxis(np.asarray(x, np.float32).astype(ml_dtypes.bfloat16).astype(np.float64), axis, -1)
    blocks = v.reshape(v.shape[:-1] + (-1, 32))
    amax = np.abs(blocks).max(-1, keepdims=True)
    byte = np.maximum(np.where(amax > 0, np.frexp(amax)[1] - 1 + 127, 0) - down, 1)
    scale = np.exp2(byte - 127.0)
    codes = (blocks / scale).astype(np.float32).astype(dtype).astype(np.float64)
    return np.moveaxis((codes * scale).reshape(v.shape), -1, axis)


WIDE = False


def mx_kscale(k):
    if not WIDE:
        return np.ones(k)
    levels = np.array([10, -10, 5, -5, 0])
    a = np.random.permutation(np.resize(levels, k // 512 * 4)).reshape(k // 512, 4)
    idx = np.arange(k)
    return np.exp2(a[idx // 512, idx % 128 // 32])


BF16 = ml_dtypes.bfloat16


def bf(x):
    return np.asarray(x, np.float32).astype(BF16)


def f64(x):
    return np.asarray(x).astype(np.float64)


B, GH, GW, F_IN, F_OUT = 2, 16, 16, 16384, 512


def setup_inputs():
    s = mx_kscale(F_IN)
    return {"X": bf(np.random.standard_normal((B, GH * GW, F_IN)) * s),
            "W_gcn": bf(np.random.standard_normal((F_IN, F_OUT)) * 0.5 / np.sqrt(F_IN) / s[:, None]),
            "b": bf(np.random.standard_normal(F_OUT) * 0.3),
            "H": GH, "Wd": GW}


def _neighbor_sum(Xg):
    p = np.pad(Xg, ((0, 0), (1, 1), (1, 1), (0, 0)))
    return (p[:, :-2, 1:-1] + p[:, 2:, 1:-1]
            + p[:, 1:-1, :-2] + p[:, 1:-1, 2:])


def reference(X, W_gcn, b, H, Wd):
    X = f64(X)
    Bn, N, F = X.shape
    Xg = X.reshape(Bn, H, Wd, F)
    AX = _neighbor_sum(Xg).reshape(Bn, N, F)
    return (mxq(AX, 2, "e4m3") @ mxq(f64(W_gcn), 0, "e4m3")) + f64(b)

@@ -1,0 +1,201 @@
+from contextlib import ExitStack
+
+import concourse.masks as masks
+import concourse.mybir as mybir
+
+BF16 = mybir.dt.bfloat16
+F32 = mybir.dt.float32
+U32 = mybir.dt.uint32
+U8 = mybir.dt.uint8
+FP8X4 = mybir.dt.float8_e4m3fn_x4
+ADD = mybir.AluOpType.add
+
+P = 128
+PACK = 4
+K_PASS = P * PACK
+BATCH = 2
+GRID = 16
+NODES = BATCH * GRID * GRID
+F_IN = 16384
+F_OUT = 512
+PASSES = F_IN // K_PASS
+NODE_TILES = NODES // P
+CHUNK_PASSES = 2
+CHUNKS = PASSES // CHUNK_PASSES
+CHUNK_F = CHUNK_PASSES * K_PASS
+PAD = GRID + 2
+SUMS = GRID + 1
+
+FLOPS = 2 * NODES * F_IN * F_OUT + 3 * NODES * F_IN + NODES * F_OUT
+
+
+def tile_graphconvlayer_k_kernel(tc, X, W_gcn, b, H, Wd, out):
+    nc = tc.nc
+    assert H == GRID and Wd == GRID
+
+    x_rows = X.rearrange("b n f -> (b n) f").rearrange("(r p) f -> p r f", p=P)
+    out_rows = out.rearrange("b n o -> (b n) o")
+
+    with ExitStack() as ctx:
+        const = ctx.enter_context(tc.tile_pool(name="const", bufs=1))
+        loads = ctx.enter_context(tc.tile_pool(name="loads", bufs=4))
+        work = ctx.enter_context(tc.tile_pool(name="work", bufs=2))
+        quant = ctx.enter_context(tc.tile_pool(name="quant", bufs=3))
+        acc_pool = ctx.enter_context(tc.psum_pool(name="acc", bufs=1))
+        xt_pool = ctx.enter_context(tc.psum_pool(name="xt", bufs=4))
+
+        ident = const.tile([P, P], F32, name="ident")
+        masks.make_identity(nc, ident[:])
+
+        bordered = [
+            const.tile([P, BATCH, PAD, PAD * PACK], BF16, name="bordered%d" % s) for s in range(3)
+        ]
+        for s in range(3):
+            nc.vector.memset(bordered[s][:], 0.0)
+
+        acc = [acc_pool.tile([P, F_OUT], F32, name="acc%d" % r) for r in range(NODE_TILES)]
+        bias = const.tile([P, F_OUT], BF16, name="bias")
+
+        x_chunk = {}
+        w_chunk = {}
+        pair_sums = {}
+        ax_grouped = {}
+        ax_codes = {}
+        ax_scales = {}
+        w_grouped = {}
+        w_codes = {}
+        w_scales = {}
+
+        def load(c):
+            x_sb = loads.tile([P, NODE_TILES, CHUNK_F], BF16, name="x_sb")
+            nc.sync.dma_start(out=x_sb[:], in_=x_rows[:, :, c * CHUNK_F : (c + 1) * CHUNK_F])
+            x_chunk[c] = x_sb
+            w_sb = loads.tile([P, 2 * CHUNK_PASSES, 2 * F_OUT], BF16, name="w_sb")
+            nc.sync.dma_start(
+                out=w_sb[:],
+                in_=W_gcn[c * CHUNK_F : (c + 1) * CHUNK_F, :].rearrange(
+                    "(s p e) o -> p s (e o)", p=P, e=2
+                ),
+            )
+            w_chunk[c] = w_sb
+
+        def transpose_x(g):
+            c, local = divmod(g, CHUNK_PASSES)
+            words = x_chunk[c][:].bitcast(F32)
+            for bb in range(BATCH):
+                xt = xt_pool.tile([P, 2, GRID * GRID], F32, name="xt")
+                for u in range(2):
+                    for half in range(2):
+                        first = local * (K_PASS // 2) + u * P
+                        nc.tensor.transpose(
+                            xt[:, u, half * P : (half + 1) * P],
+                            words[:, 2 * bb + half, first : first + P],
+                            ident[:],
+                        )
+                inner = bordered[g % 3][:].bitcast(F32)[:, bb, 1 : 1 + GRID, 2 : 2 + 2 * GRID]
+                nc.scalar.copy(
+                    out=inner.rearrange("p i (j u) -> p i j u", u=2),
+                    in_=xt[:].rearrange("p u (i j) -> p i j u", j=GRID),
+                )
+
+        def regroup_w(g):
+            c, local = divmod(g, CHUNK_PASSES)
+            rows = w_chunk[c][:, 2 * local : 2 * local + 2, :].rearrange(
+                "p u (e o) -> p (u e) o", e=2
+            )
+            grouped = work.tile([P, F_OUT, PACK], BF16, name="w_grouped", align_bytes=64)
+            nc.scalar.copy(
+                out=grouped[:].rearrange("p (c i) t -> p c t i", i=4),
+                in_=rows.rearrange("p t (c i) -> p c t i", i=4),
+            )
+            w_grouped[g] = grouped
+
+        def quantise_w(g):
+            codes = quant.tile([P, F_OUT], U32, name="w_codes", align_bytes=64)
+            scales = quant.tile([P, F_OUT], U8, name="w_scales", align_bytes=64)
+            nc.vector.quantize_mx(
+                out=codes[:].bitcast(FP8X4),
+                scales=scales[:],
+                in_=w_grouped[g][:].rearrange("p o t -> p (o t)"),
+            )
+            w_codes[g] = codes
+            w_scales[g] = scales
+
+        def add_pairs(g):
+            src = bordered[g % 3]
+            pair = work.tile([P, BATCH, SUMS, SUMS * PACK], F32, name="pair")
+            nc.vector.tensor_tensor(
+                out=pair[:],
+                in0=src[:, :, 0:SUMS, PACK : PACK + SUMS * PACK],
+                in1=src[:, :, 1 : 1 + SUMS, 0 : SUMS * PACK],
+                op=ADD,
+            )
+            pair_sums[g] = pair
+
+        def add_sums(g):
+            pair = pair_sums[g]
+            grouped = work.tile([P, BATCH, GRID, GRID * PACK], BF16, name="ax_grouped", align_bytes=64)
+            nc.vector.tensor_tensor(
+                out=grouped[:],
+                in0=pair[:, :, 0:GRID, 0 : GRID * PACK],
+                in1=pair[:, :, 1 : 1 + GRID, PACK : PACK + GRID * PACK],
+                op=ADD,
+            )
+            ax_grouped[g] = grouped
+
+        def quantise_ax(g):
+            codes = quant.tile([P, NODES], U32, name="ax_codes", align_bytes=64)
+            scales = quant.tile([P, NODES], U8, name="ax_scales", align_bytes=64)
+            nc.vector.quantize_mx(
+                out=codes[:].bitcast(FP8X4),
+                scales=scales[:],
+                in_=ax_grouped[g][:].rearrange("p b i c -> p (b i c)"),
+            )
+            ax_codes[g] = codes
+            ax_scales[g] = scales
+
+        def multiply(g):
+            for r in range(NODE_TILES):
+                nodes = slice(r * P, (r + 1) * P)
+                nc.tensor.matmul_mx(
+                    out=acc[r][:],
+                    lhsT=ax_codes[g][:, nodes].bitcast(FP8X4),
+                    lhsT_scale=ax_scales[g][:, nodes],
+                    rhs=w_codes[g][:].bitcast(FP8X4),
+                    rhs_scale=w_scales[g][:],
+                    start=(g == 0),
+                    stop=(g == PASSES - 1),
+                )
+
+        def prepare(g):
+            c, local = divmod(g, CHUNK_PASSES)
+            if local == 0 and c + 3 < CHUNKS:
+                load(c + 3)
+            transpose_x(g)
+            regroup_w(g)
+
+        with tc.manual_schedule():
+            for c in range(3):
+                load(c)
+            prepare(0)
+            add_pairs(0)
+            quantise_w(0)
+            prepare(1)
+            nc.sync.dma_start(out=bias[:], in_=b.partition_broadcast(P))
+            for g in range(PASSES):
+                if g + 2 < PASSES:
+                    prepare(g + 2)
+                add_sums(g)
+                if g >= 1:
+                    quantise_ax(g - 1)
+                    multiply(g - 1)
+                if g + 1 < PASSES:
+                    add_pairs(g + 1)
+                    quantise_w(g + 1)
+            quantise_ax(PASSES - 1)
+            multiply(PASSES - 1)
+
+            for r in range(NODE_TILES):
+                result = work.tile([P, F_OUT], F32, name="result")
+                nc.vector.tensor_tensor(out=result[:], in0=acc[r][:], in1=bias[:], op=ADD)
+                nc.sync.dma_start(out=out_rows[r * P : (r + 1) * P, :], in_=result[:])

@@ -25,8 +25,13 @@ CHUNKS = PASSES // CHUNK_PASSES
 CHUNK_F = CHUNK_PASSES * K_PASS
 PAD = GRID + 2
 SUMS = GRID + 1
+MID_FIRST = 64
 
 FLOPS = 2 * NODES * F_IN * F_OUT + 3 * NODES * F_IN + NODES * F_OUT
+
+
+def sums_on_tensor(g):
+    return (3 * g) % 8 < 3
 
 
 def tile_graphconvlayer_k_kernel(tc, X, W_gcn, b, H, Wd, out):
@@ -53,10 +58,31 @@ def tile_graphconvlayer_k_kernel(tc, X, W_gcn, b, H, Wd, out):
         for s in range(3):
             nc.vector.memset(bordered[s][:], 0.0)
 
+        wide = const.tile([P, P + 2 * GRID], BF16, name="wide")
+        nc.vector.memset(wide[:], 0.0)
+        nc.vector.tensor_copy(out=wide[:, GRID : GRID + P], in_=ident[:])
+        adjacency = const.tile([P, P], BF16, name="adjacency")
+        nc.vector.tensor_tensor(
+            out=adjacency[:], in0=wide[:, 0:P], in1=wide[:, 2 * GRID : 2 * GRID + P], op=ADD
+        )
+        by_row = adjacency[:].rearrange("p (i j) -> p i j", j=GRID)
+        from_left = wide[:, GRID - 1 : GRID - 1 + P].rearrange("p (i j) -> p i j", j=GRID)
+        from_right = wide[:, GRID + 1 : GRID + 1 + P].rearrange("p (i j) -> p i j", j=GRID)
+        nc.vector.tensor_tensor(
+            out=by_row[:, :, 1:GRID], in0=by_row[:, :, 1:GRID], in1=from_left[:, :, 1:GRID], op=ADD
+        )
+        nc.vector.tensor_tensor(
+            out=by_row[:, :, 0 : GRID - 1],
+            in0=by_row[:, :, 0 : GRID - 1],
+            in1=from_right[:, :, 0 : GRID - 1],
+            op=ADD,
+        )
+
         acc = [acc_pool.tile([P, F_OUT], F32, name="acc%d" % r) for r in range(NODE_TILES)]
         bias = const.tile([P, F_OUT], BF16, name="bias")
 
         x_chunk = {}
+        x_middle = {}
         w_chunk = {}
         pair_sums = {}
         ax_grouped = {}
@@ -78,6 +104,16 @@ def tile_graphconvlayer_k_kernel(tc, X, W_gcn, b, H, Wd, out):
                 ),
             )
             w_chunk[c] = w_sb
+            for g in range(c * CHUNK_PASSES, (c + 1) * CHUNK_PASSES):
+                if sums_on_tensor(g):
+                    x_mid = loads.tile([P, BATCH, K_PASS], BF16, name="x_mid")
+                    nc.sync.dma_start(
+                        out=x_mid[:],
+                        in_=X[:, MID_FIRST : MID_FIRST + P, g * K_PASS : (g + 1) * K_PASS].rearrange(
+                            "b p f -> p b f"
+                        ),
+                    )
+                    x_middle[g] = x_mid
 
         def transpose_x(g):
             c, local = divmod(g, CHUNK_PASSES)
@@ -97,6 +133,37 @@ def tile_graphconvlayer_k_kernel(tc, X, W_gcn, b, H, Wd, out):
                     out=inner.rearrange("p i (j u) -> p i j u", u=2),
                     in_=xt[:].rearrange("p u (i j) -> p i j u", j=GRID),
                 )
+
+        def sum_on_tensor(g):
+            c, local = divmod(g, CHUNK_PASSES)
+            grouped = work.tile([P, NODES * PACK], BF16, name="ax_plain", align_bytes=64)
+            edge = P - GRID
+            for bb in range(BATCH):
+                upper = xt_pool.tile([P, PACK, P], F32, name="xt")
+                lower = xt_pool.tile([P, PACK, P], F32, name="xt")
+                for t in range(PACK):
+                    first = (t // 2) * (K_PASS // 2) + t % 2
+                    last = (t // 2 + 1) * (K_PASS // 2)
+                    here = local * K_PASS
+                    x_up = x_chunk[c][:, 2 * bb, here + first : here + last : 2]
+                    x_mid = x_middle[g][:, bb, first:last:2]
+                    x_low = x_chunk[c][:, 2 * bb + 1, here + first : here + last : 2]
+                    for dst, lhsT, columns in (
+                        (upper[:, t, 0:edge], x_up, adjacency[:, 0:edge]),
+                        (upper[:, t, edge:P], x_mid, adjacency[:, 3 * GRID : 4 * GRID]),
+                        (lower[:, t, 0:GRID], x_mid, adjacency[:, 4 * GRID : 5 * GRID]),
+                        (lower[:, t, GRID:P], x_low, adjacency[:, GRID:P]),
+                    ):
+                        nc.tensor.matmul(out=dst, lhsT=lhsT, rhs=columns, start=True, stop=True)
+                for half, bank in enumerate((upper, lower)):
+                    r = 2 * bb + half
+                    nc.scalar.copy(
+                        out=grouped[:, r * P * PACK : (r + 1) * P * PACK].rearrange(
+                            "p (n t) -> p n t", t=PACK
+                        ),
+                        in_=bank[:].rearrange("p t n -> p n t"),
+                    )
+            ax_grouped[g] = grouped[:]
 
         def regroup_w(g):
             c, local = divmod(g, CHUNK_PASSES)
@@ -141,7 +208,7 @@ def tile_graphconvlayer_k_kernel(tc, X, W_gcn, b, H, Wd, out):
                 in1=pair[:, :, 1 : 1 + GRID, PACK : PACK + GRID * PACK],
                 op=ADD,
             )
-            ax_grouped[g] = grouped
+            ax_grouped[g] = grouped[:].rearrange("p b i c -> p (b i c)")
 
         def quantise_ax(g):
             codes = quant.tile([P, NODES], U32, name="ax_codes", align_bytes=64)
@@ -149,7 +216,7 @@ def tile_graphconvlayer_k_kernel(tc, X, W_gcn, b, H, Wd, out):
             nc.vector.quantize_mx(
                 out=codes[:].bitcast(FP8X4),
                 scales=scales[:],
-                in_=ax_grouped[g][:].rearrange("p b i c -> p (b i c)"),
+                in_=ax_grouped[g],
             )
             ax_codes[g] = codes
             ax_scales[g] = scales
@@ -171,26 +238,30 @@ def tile_graphconvlayer_k_kernel(tc, X, W_gcn, b, H, Wd, out):
             c, local = divmod(g, CHUNK_PASSES)
             if local == 0 and c + 3 < CHUNKS:
                 load(c + 3)
-            transpose_x(g)
+            if sums_on_tensor(g):
+                sum_on_tensor(g)
+            else:
+                transpose_x(g)
             regroup_w(g)
 
         with tc.manual_schedule():
             for c in range(3):
                 load(c)
             prepare(0)
-            add_pairs(0)
             quantise_w(0)
             prepare(1)
             nc.sync.dma_start(out=bias[:], in_=b.partition_broadcast(P))
             for g in range(PASSES):
                 if g + 2 < PASSES:
                     prepare(g + 2)
-                add_sums(g)
+                if not sums_on_tensor(g):
+                    add_sums(g)
                 if g >= 1:
                     quantise_ax(g - 1)
                     multiply(g - 1)
                 if g + 1 < PASSES:
-                    add_pairs(g + 1)
+                    if not sums_on_tensor(g + 1):
+                        add_pairs(g + 1)
                     quantise_w(g + 1)
             quantise_ax(PASSES - 1)
             multiply(PASSES - 1)

@@ -20,9 +20,7 @@ F_IN = 16384
 F_OUT = 512
 PASSES = F_IN // K_PASS
 NODE_TILES = NODES // P
-CHUNK_PASSES = 2
-CHUNKS = PASSES // CHUNK_PASSES
-CHUNK_F = CHUNK_PASSES * K_PASS
+LOADS_AHEAD = 6
 PAD = GRID + 2
 SUMS = GRID + 1
 MID_FIRST = 64
@@ -31,7 +29,7 @@ FLOPS = 2 * NODES * F_IN * F_OUT + 3 * NODES * F_IN + NODES * F_OUT
 
 
 def sums_on_tensor(g):
-    return (3 * g) % 8 < 3
+    return (3 * g + 5) % 8 < 3
 
 
 def tile_graphconvlayer_k_kernel(tc, X, W_gcn, b, H, Wd, out):
@@ -43,8 +41,9 @@ def tile_graphconvlayer_k_kernel(tc, X, W_gcn, b, H, Wd, out):
 
     with ExitStack() as ctx:
         const = ctx.enter_context(tc.tile_pool(name="const", bufs=1))
-        loads = ctx.enter_context(tc.tile_pool(name="loads", bufs=4))
+        loads = ctx.enter_context(tc.tile_pool(name="loads", bufs=LOADS_AHEAD + 2))
         work = ctx.enter_context(tc.tile_pool(name="work", bufs=2))
+        regrouped = ctx.enter_context(tc.tile_pool(name="regrouped", bufs=3))
         quant = ctx.enter_context(tc.tile_pool(name="quant", bufs=3))
         acc_pool = ctx.enter_context(tc.psum_pool(name="acc", bufs=1))
         xt_pool = ctx.enter_context(tc.psum_pool(name="xt", bufs=4))
@@ -81,9 +80,9 @@ def tile_graphconvlayer_k_kernel(tc, X, W_gcn, b, H, Wd, out):
         acc = [acc_pool.tile([P, F_OUT], F32, name="acc%d" % r) for r in range(NODE_TILES)]
         bias = const.tile([P, F_OUT], BF16, name="bias")
 
-        x_chunk = {}
+        x_pass = {}
         x_middle = {}
-        w_chunk = {}
+        w_pass = {}
         pair_sums = {}
         ax_grouped = {}
         ax_codes = {}
@@ -92,40 +91,34 @@ def tile_graphconvlayer_k_kernel(tc, X, W_gcn, b, H, Wd, out):
         w_codes = {}
         w_scales = {}
 
-        def load(c):
-            x_sb = loads.tile([P, NODE_TILES, CHUNK_F], BF16, name="x_sb")
-            nc.sync.dma_start(out=x_sb[:], in_=x_rows[:, :, c * CHUNK_F : (c + 1) * CHUNK_F])
-            x_chunk[c] = x_sb
-            w_sb = loads.tile([P, 2 * CHUNK_PASSES, 2 * F_OUT], BF16, name="w_sb")
+        def load(g):
+            features = slice(g * K_PASS, (g + 1) * K_PASS)
+            x_sb = loads.tile([P, NODE_TILES, K_PASS], BF16, name="x_sb")
+            nc.sync.dma_start(out=x_sb[:], in_=x_rows[:, :, features])
+            x_pass[g] = x_sb
+            if sums_on_tensor(g):
+                x_mid = loads.tile([P, BATCH, K_PASS], BF16, name="x_mid")
+                nc.sync.dma_start(
+                    out=x_mid[:],
+                    in_=X[:, MID_FIRST : MID_FIRST + P, features].rearrange("b p f -> p b f"),
+                )
+                x_middle[g] = x_mid
+            w_sb = loads.tile([P, 2, 2 * F_OUT], BF16, name="w_sb")
             nc.sync.dma_start(
                 out=w_sb[:],
-                in_=W_gcn[c * CHUNK_F : (c + 1) * CHUNK_F, :].rearrange(
-                    "(s p e) o -> p s (e o)", p=P, e=2
-                ),
+                in_=W_gcn[features, :].rearrange("(u p e) o -> p u (e o)", p=P, e=2),
             )
-            w_chunk[c] = w_sb
-            for g in range(c * CHUNK_PASSES, (c + 1) * CHUNK_PASSES):
-                if sums_on_tensor(g):
-                    x_mid = loads.tile([P, BATCH, K_PASS], BF16, name="x_mid")
-                    nc.sync.dma_start(
-                        out=x_mid[:],
-                        in_=X[:, MID_FIRST : MID_FIRST + P, g * K_PASS : (g + 1) * K_PASS].rearrange(
-                            "b p f -> p b f"
-                        ),
-                    )
-                    x_middle[g] = x_mid
+            w_pass[g] = w_sb
 
         def transpose_x(g):
-            c, local = divmod(g, CHUNK_PASSES)
-            words = x_chunk[c][:].bitcast(F32)
+            words = x_pass[g][:].bitcast(F32)
             for bb in range(BATCH):
                 xt = xt_pool.tile([P, 2, GRID * GRID], F32, name="xt")
                 for u in range(2):
                     for half in range(2):
-                        first = local * (K_PASS // 2) + u * P
                         nc.tensor.transpose(
                             xt[:, u, half * P : (half + 1) * P],
-                            words[:, 2 * bb + half, first : first + P],
+                            words[:, 2 * bb + half, u * P : (u + 1) * P],
                             ident[:],
                         )
                 inner = bordered[g % 3][:].bitcast(F32)[:, bb, 1 : 1 + GRID, 2 : 2 + 2 * GRID]
@@ -135,7 +128,6 @@ def tile_graphconvlayer_k_kernel(tc, X, W_gcn, b, H, Wd, out):
                 )
 
         def sum_on_tensor(g):
-            c, local = divmod(g, CHUNK_PASSES)
             grouped = work.tile([P, NODES * PACK], BF16, name="ax_plain", align_bytes=64)
             edge = P - GRID
             for bb in range(BATCH):
@@ -144,10 +136,9 @@ def tile_graphconvlayer_k_kernel(tc, X, W_gcn, b, H, Wd, out):
                 for t in range(PACK):
                     first = (t // 2) * (K_PASS // 2) + t % 2
                     last = (t // 2 + 1) * (K_PASS // 2)
-                    here = local * K_PASS
-                    x_up = x_chunk[c][:, 2 * bb, here + first : here + last : 2]
+                    x_up = x_pass[g][:, 2 * bb, first:last:2]
                     x_mid = x_middle[g][:, bb, first:last:2]
-                    x_low = x_chunk[c][:, 2 * bb + 1, here + first : here + last : 2]
+                    x_low = x_pass[g][:, 2 * bb + 1, first:last:2]
                     for dst, lhsT, columns in (
                         (upper[:, t, 0:edge], x_up, adjacency[:, 0:edge]),
                         (upper[:, t, edge:P], x_mid, adjacency[:, 3 * GRID : 4 * GRID]),
@@ -166,11 +157,8 @@ def tile_graphconvlayer_k_kernel(tc, X, W_gcn, b, H, Wd, out):
             ax_grouped[g] = grouped[:]
 
         def regroup_w(g):
-            c, local = divmod(g, CHUNK_PASSES)
-            rows = w_chunk[c][:, 2 * local : 2 * local + 2, :].rearrange(
-                "p u (e o) -> p (u e) o", e=2
-            )
-            grouped = work.tile([P, F_OUT, PACK], BF16, name="w_grouped", align_bytes=64)
+            rows = w_pass[g][:].rearrange("p u (e o) -> p (u e) o", e=2)
+            grouped = regrouped.tile([P, F_OUT, PACK], BF16, name="w_grouped", align_bytes=64)
             nc.scalar.copy(
                 out=grouped[:].rearrange("p (c i) t -> p c t i", i=4),
                 in_=rows.rearrange("p t (c i) -> p c t i", i=4),
@@ -235,9 +223,8 @@ def tile_graphconvlayer_k_kernel(tc, X, W_gcn, b, H, Wd, out):
                 )
 
         def prepare(g):
-            c, local = divmod(g, CHUNK_PASSES)
-            if local == 0 and c + 3 < CHUNKS:
-                load(c + 3)
+            if g + LOADS_AHEAD < PASSES:
+                load(g + LOADS_AHEAD)
             if sums_on_tensor(g):
                 sum_on_tensor(g)
             else:
@@ -245,9 +232,10 @@ def tile_graphconvlayer_k_kernel(tc, X, W_gcn, b, H, Wd, out):
             regroup_w(g)
 
         with tc.manual_schedule():
-            for c in range(3):
-                load(c)
+            for g in range(LOADS_AHEAD):
+                load(g)
             prepare(0)
+            add_pairs(0)
             quantise_w(0)
             prepare(1)
             nc.sync.dma_start(out=bias[:], in_=b.partition_broadcast(P))

@@ -21,7 +21,6 @@ F_OUT = 512
 PASSES = F_IN // K_PASS
 NODE_TILES = NODES // P
 LOADS_AHEAD = 6
-PAD = GRID + 2
 SUMS = GRID + 1
 MID_FIRST = 64
 
@@ -52,7 +51,7 @@ def tile_graphconvlayer_k_kernel(tc, X, W_gcn, b, H, Wd, out):
         masks.make_identity(nc, ident[:])
 
         bordered = [
-            const.tile([P, BATCH, PAD, PAD * PACK], BF16, name="bordered%d" % s) for s in range(3)
+            const.tile([P, BATCH, SUMS, SUMS * PACK], BF16, name="bordered%d" % s) for s in range(3)
         ]
         for s in range(3):
             nc.vector.memset(bordered[s][:], 0.0)
@@ -82,6 +81,7 @@ def tile_graphconvlayer_k_kernel(tc, X, W_gcn, b, H, Wd, out):
 
         x_pass = {}
         x_middle = {}
+        xt_banks = {}
         w_pass = {}
         pair_sums = {}
         ax_grouped = {}
@@ -112,20 +112,21 @@ def tile_graphconvlayer_k_kernel(tc, X, W_gcn, b, H, Wd, out):
 
         def transpose_x(g):
             words = x_pass[g][:].bitcast(F32)
+            xt_banks[g] = []
             for bb in range(BATCH):
-                xt = xt_pool.tile([P, 2, GRID * GRID], F32, name="xt")
+                xt = xt_pool.tile([P, GRID * GRID, 2], F32, name="xt")
                 for u in range(2):
                     for half in range(2):
                         nc.tensor.transpose(
-                            xt[:, u, half * P : (half + 1) * P],
+                            xt[:, half * P : (half + 1) * P, u],
                             words[:, 2 * bb + half, u * P : (u + 1) * P],
                             ident[:],
                         )
-                inner = bordered[g % 3][:].bitcast(F32)[:, bb, 1 : 1 + GRID, 2 : 2 + 2 * GRID]
                 nc.scalar.copy(
-                    out=inner.rearrange("p i (j u) -> p i j u", u=2),
-                    in_=xt[:].rearrange("p u (i j) -> p i j u", j=GRID),
+                    out=bordered[g % 3][:].bitcast(F32)[:, bb, 0:GRID, 2 : 2 + 2 * GRID],
+                    in_=xt[:].rearrange("p (i j) u -> p i (j u)", j=GRID),
                 )
+                xt_banks[g].append(xt)
 
         def sum_on_tensor(g):
             grouped = work.tile([P, NODES * PACK], BF16, name="ax_plain", align_bytes=64)
@@ -178,24 +179,27 @@ def tile_graphconvlayer_k_kernel(tc, X, W_gcn, b, H, Wd, out):
 
         def add_pairs(g):
             src = bordered[g % 3]
+            inner = GRID * PACK
             pair = work.tile([P, BATCH, SUMS, SUMS * PACK], F32, name="pair")
-            nc.vector.tensor_tensor(
-                out=pair[:],
-                in0=src[:, :, 0:SUMS, PACK : PACK + SUMS * PACK],
-                in1=src[:, :, 1 : 1 + SUMS, 0 : SUMS * PACK],
-                op=ADD,
-            )
+            nc.vector.tensor_copy(out=pair[:, :, 0, :], in_=src[:, :, 0, :])
+            nc.vector.tensor_copy(out=pair[:, :, 1:SUMS, inner:], in_=src[:, :, 1:SUMS, inner:])
+            for bb in range(BATCH):
+                above = xt_banks[g][bb][:].bitcast(BF16).rearrange("p (i j) t -> p i (j t)", j=GRID)
+                nc.vector.tensor_tensor(
+                    out=pair[:, bb, 1:SUMS, 0:inner], in0=above, in1=src[:, bb, 1:SUMS, 0:inner], op=ADD
+                )
             pair_sums[g] = pair
 
         def add_sums(g):
             pair = pair_sums[g]
             grouped = work.tile([P, BATCH, GRID, GRID * PACK], BF16, name="ax_grouped", align_bytes=64)
-            nc.vector.tensor_tensor(
-                out=grouped[:],
-                in0=pair[:, :, 0:GRID, 0 : GRID * PACK],
-                in1=pair[:, :, 1 : 1 + GRID, PACK : PACK + GRID * PACK],
-                op=ADD,
-            )
+            for bb, engine in enumerate((nc.gpsimd, nc.vector)):
+                engine.tensor_tensor(
+                    out=grouped[:, bb],
+                    in0=pair[:, bb, 0:GRID, 0 : GRID * PACK],
+                    in1=pair[:, bb, 1 : 1 + GRID, PACK : PACK + GRID * PACK],
+                    op=ADD,
+                )
             ax_grouped[g] = grouped[:].rearrange("p b i c -> p (b i c)")
 
         def quantise_ax(g):
@@ -226,10 +230,11 @@ def tile_graphconvlayer_k_kernel(tc, X, W_gcn, b, H, Wd, out):
             if g + LOADS_AHEAD < PASSES:
                 load(g + LOADS_AHEAD)
             if sums_on_tensor(g):
+                regroup_w(g)
                 sum_on_tensor(g)
             else:
                 transpose_x(g)
-            regroup_w(g)
+                regroup_w(g)
 
         with tc.manual_schedule():
             for g in range(LOADS_AHEAD):
@@ -240,13 +245,13 @@ def tile_graphconvlayer_k_kernel(tc, X, W_gcn, b, H, Wd, out):
             prepare(1)
             nc.sync.dma_start(out=bias[:], in_=b.partition_broadcast(P))
             for g in range(PASSES):
-                if g + 2 < PASSES:
-                    prepare(g + 2)
                 if not sums_on_tensor(g):
                     add_sums(g)
                 if g >= 1:
                     quantise_ax(g - 1)
                     multiply(g - 1)
+                if g + 2 < PASSES:
+                    prepare(g + 2)
                 if g + 1 < PASSES:
                     if not sums_on_tensor(g + 1):
                         add_pairs(g + 1)

@@ -21,6 +21,7 @@ F_OUT = 512
 PASSES = F_IN // K_PASS
 NODE_TILES = NODES // P
 LOADS_AHEAD = 6
+PAD = GRID + 2
 SUMS = GRID + 1
 MID_FIRST = 64
 
@@ -28,7 +29,7 @@ FLOPS = 2 * NODES * F_IN * F_OUT + 3 * NODES * F_IN + NODES * F_OUT
 
 
 def sums_on_tensor(g):
-    return (3 * g + 5) % 8 < 3
+    return (3 * g + 3) % 8 < 3
 
 
 def tile_graphconvlayer_k_kernel(tc, X, W_gcn, b, H, Wd, out):
@@ -51,7 +52,7 @@ def tile_graphconvlayer_k_kernel(tc, X, W_gcn, b, H, Wd, out):
         masks.make_identity(nc, ident[:])
 
         bordered = [
-            const.tile([P, BATCH, SUMS, SUMS * PACK], BF16, name="bordered%d" % s) for s in range(3)
+            const.tile([P, BATCH, PAD, PAD * PACK], BF16, name="bordered%d" % s) for s in range(3)
         ]
         for s in range(3):
             nc.vector.memset(bordered[s][:], 0.0)
@@ -81,7 +82,6 @@ def tile_graphconvlayer_k_kernel(tc, X, W_gcn, b, H, Wd, out):
 
         x_pass = {}
         x_middle = {}
-        xt_banks = {}
         w_pass = {}
         pair_sums = {}
         ax_grouped = {}
@@ -112,21 +112,20 @@ def tile_graphconvlayer_k_kernel(tc, X, W_gcn, b, H, Wd, out):
 
         def transpose_x(g):
             words = x_pass[g][:].bitcast(F32)
-            xt_banks[g] = []
             for bb in range(BATCH):
-                xt = xt_pool.tile([P, GRID * GRID, 2], F32, name="xt")
+                xt = xt_pool.tile([P, 2, GRID * GRID], F32, name="xt")
                 for u in range(2):
                     for half in range(2):
                         nc.tensor.transpose(
-                            xt[:, half * P : (half + 1) * P, u],
+                            xt[:, u, half * P : (half + 1) * P],
                             words[:, 2 * bb + half, u * P : (u + 1) * P],
                             ident[:],
                         )
+                inner = bordered[g % 3][:].bitcast(F32)[:, bb, 1 : 1 + GRID, 2 : 2 + 2 * GRID]
                 nc.scalar.copy(
-                    out=bordered[g % 3][:].bitcast(F32)[:, bb, 0:GRID, 2 : 2 + 2 * GRID],
-                    in_=xt[:].rearrange("p (i j) u -> p i (j u)", j=GRID),
+                    out=inner.rearrange("p i (j u) -> p i j u", u=2),
+                    in_=xt[:].rearrange("p u (i j) -> p i j u", j=GRID),
                 )
-                xt_banks[g].append(xt)
 
         def sum_on_tensor(g):
             grouped = work.tile([P, NODES * PACK], BF16, name="ax_plain", align_bytes=64)
@@ -179,27 +178,24 @@ def tile_graphconvlayer_k_kernel(tc, X, W_gcn, b, H, Wd, out):
 
         def add_pairs(g):
             src = bordered[g % 3]
-            inner = GRID * PACK
             pair = work.tile([P, BATCH, SUMS, SUMS * PACK], F32, name="pair")
-            nc.vector.tensor_copy(out=pair[:, :, 0, :], in_=src[:, :, 0, :])
-            nc.vector.tensor_copy(out=pair[:, :, 1:SUMS, inner:], in_=src[:, :, 1:SUMS, inner:])
-            for bb in range(BATCH):
-                above = xt_banks[g][bb][:].bitcast(BF16).rearrange("p (i j) t -> p i (j t)", j=GRID)
-                nc.vector.tensor_tensor(
-                    out=pair[:, bb, 1:SUMS, 0:inner], in0=above, in1=src[:, bb, 1:SUMS, 0:inner], op=ADD
-                )
+            nc.vector.tensor_tensor(
+                out=pair[:],
+                in0=src[:, :, 0:SUMS, PACK : PACK + SUMS * PACK],
+                in1=src[:, :, 1 : 1 + SUMS, 0 : SUMS * PACK],
+                op=ADD,
+            )
             pair_sums[g] = pair
 
         def add_sums(g):
             pair = pair_sums[g]
             grouped = work.tile([P, BATCH, GRID, GRID * PACK], BF16, name="ax_grouped", align_bytes=64)
-            for bb, engine in enumerate((nc.gpsimd, nc.vector)):
-                engine.tensor_tensor(
-                    out=grouped[:, bb],
-                    in0=pair[:, bb, 0:GRID, 0 : GRID * PACK],
-                    in1=pair[:, bb, 1 : 1 + GRID, PACK : PACK + GRID * PACK],
-                    op=ADD,
-                )
+            nc.vector.tensor_tensor(
+                out=grouped[:],
+                in0=pair[:, :, 0:GRID, 0 : GRID * PACK],
+                in1=pair[:, :, 1 : 1 + GRID, PACK : PACK + GRID * PACK],
+                op=ADD,
+            )
             ax_grouped[g] = grouped[:].rearrange("p b i c -> p (b i c)")
 
         def quantise_ax(g):
@@ -245,13 +241,13 @@ def tile_graphconvlayer_k_kernel(tc, X, W_gcn, b, H, Wd, out):
             prepare(1)
             nc.sync.dma_start(out=bias[:], in_=b.partition_broadcast(P))
             for g in range(PASSES):
+                if g + 2 < PASSES:
+                    prepare(g + 2)
                 if not sums_on_tensor(g):
                     add_sums(g)
                 if g >= 1:
                     quantise_ax(g - 1)
                     multiply(g - 1)
-                if g + 2 < PASSES:
-                    prepare(g + 2)
                 if g + 1 < PASSES:
                     if not sums_on_tensor(g + 1):
                         add_pairs(g + 1)

@@ -21,7 +21,6 @@ F_OUT = 512
 PASSES = F_IN // K_PASS
 NODE_TILES = NODES // P
 LOADS_AHEAD = 6
-PAD = GRID + 2
 SUMS = GRID + 1
 MID_FIRST = 64
 
@@ -29,7 +28,7 @@ FLOPS = 2 * NODES * F_IN * F_OUT + 3 * NODES * F_IN + NODES * F_OUT
 
 
 def sums_on_tensor(g):
-    return (3 * g + 3) % 8 < 3
+    return (3 * g + 5) % 8 < 3
 
 
 def tile_graphconvlayer_k_kernel(tc, X, W_gcn, b, H, Wd, out):
@@ -52,7 +51,7 @@ def tile_graphconvlayer_k_kernel(tc, X, W_gcn, b, H, Wd, out):
         masks.make_identity(nc, ident[:])
 
         bordered = [
-            const.tile([P, BATCH, PAD, PAD * PACK], BF16, name="bordered%d" % s) for s in range(3)
+            const.tile([P, BATCH, SUMS, SUMS * PACK], BF16, name="bordered%d" % s) for s in range(3)
         ]
         for s in range(3):
             nc.vector.memset(bordered[s][:], 0.0)
@@ -82,6 +81,7 @@ def tile_graphconvlayer_k_kernel(tc, X, W_gcn, b, H, Wd, out):
 
         x_pass = {}
         x_middle = {}
+        xt_banks = {}
         w_pass = {}
         pair_sums = {}
         ax_grouped = {}
@@ -112,20 +112,21 @@ def tile_graphconvlayer_k_kernel(tc, X, W_gcn, b, H, Wd, out):
 
         def transpose_x(g):
             words = x_pass[g][:].bitcast(F32)
+            xt_banks[g] = []
             for bb in range(BATCH):
-                xt = xt_pool.tile([P, 2, GRID * GRID], F32, name="xt")
+                xt = xt_pool.tile([P, GRID * GRID, 2], F32, name="xt")
                 for u in range(2):
                     for half in range(2):
                         nc.tensor.transpose(
-                            xt[:, u, half * P : (half + 1) * P],
+                            xt[:, half * P : (half + 1) * P, u],
                             words[:, 2 * bb + half, u * P : (u + 1) * P],
                             ident[:],
                         )
-                inner = bordered[g % 3][:].bitcast(F32)[:, bb, 1 : 1 + GRID, 2 : 2 + 2 * GRID]
                 nc.scalar.copy(
-                    out=inner.rearrange("p i (j u) -> p i j u", u=2),
-                    in_=xt[:].rearrange("p u (i j) -> p i j u", j=GRID),
+                    out=bordered[g % 3][:].bitcast(F32)[:, bb, 0:GRID, 2 : 2 + 2 * GRID],
+                    in_=xt[:].rearrange("p (i j) u -> p i (j u)", j=GRID),
                 )
+                xt_banks[g].append(xt)
 
         def sum_on_tensor(g):
             grouped = work.tile([P, NODES * PACK], BF16, name="ax_plain", align_bytes=64)
@@ -178,24 +179,27 @@ def tile_graphconvlayer_k_kernel(tc, X, W_gcn, b, H, Wd, out):
 
         def add_pairs(g):
             src = bordered[g % 3]
+            inner = GRID * PACK
             pair = work.tile([P, BATCH, SUMS, SUMS * PACK], F32, name="pair")
-            nc.vector.tensor_tensor(
-                out=pair[:],
-                in0=src[:, :, 0:SUMS, PACK : PACK + SUMS * PACK],
-                in1=src[:, :, 1 : 1 + SUMS, 0 : SUMS * PACK],
-                op=ADD,
-            )
+            nc.vector.tensor_copy(out=pair[:, :, 0, :], in_=src[:, :, 0, :])
+            nc.vector.tensor_copy(out=pair[:, :, 1:SUMS, inner:], in_=src[:, :, 1:SUMS, inner:])
+            for bb in range(BATCH):
+                above = xt_banks[g][bb][:].bitcast(BF16).rearrange("p (i j) t -> p i (j t)", j=GRID)
+                nc.vector.tensor_tensor(
+                    out=pair[:, bb, 1:SUMS, 0:inner], in0=above, in1=src[:, bb, 1:SUMS, 0:inner], op=ADD
+                )
             pair_sums[g] = pair
 
         def add_sums(g):
             pair = pair_sums[g]
             grouped = work.tile([P, BATCH, GRID, GRID * PACK], BF16, name="ax_grouped", align_bytes=64)
-            nc.vector.tensor_tensor(
-                out=grouped[:],
-                in0=pair[:, :, 0:GRID, 0 : GRID * PACK],
-                in1=pair[:, :, 1 : 1 + GRID, PACK : PACK + GRID * PACK],
-                op=ADD,
-            )
+            for bb in range(BATCH):
+                nc.vector.tensor_tensor(
+                    out=grouped[:, bb],
+                    in0=pair[:, bb, 0:GRID, 0 : GRID * PACK],
+                    in1=pair[:, bb, 1 : 1 + GRID, PACK : PACK + GRID * PACK],
+                    op=ADD,
+                )
             ax_grouped[g] = grouped[:].rearrange("p b i c -> p (b i c)")
 
         def quantise_ax(g):
@@ -241,13 +245,13 @@ def tile_graphconvlayer_k_kernel(tc, X, W_gcn, b, H, Wd, out):
             prepare(1)
             nc.sync.dma_start(out=bias[:], in_=b.partition_broadcast(P))
             for g in range(PASSES):
-                if g + 2 < PASSES:
-                    prepare(g + 2)
                 if not sums_on_tensor(g):
                     add_sums(g)
                 if g >= 1:
                     quantise_ax(g - 1)
                     multiply(g - 1)
+                if g + 2 < PASSES:
+                    prepare(g + 2)
                 if g + 1 < PASSES:
                     if not sums_on_tensor(g + 1):
                         add_pairs(g + 1)

@@ -22,13 +22,14 @@ PASSES = F_IN // K_PASS
 NODE_TILES = NODES // P
 LOADS_AHEAD = 6
 SUMS = GRID + 1
+PAIR_PITCH = (SUMS + 1) * PACK
 MID_FIRST = 64
 
 FLOPS = 2 * NODES * F_IN * F_OUT + 3 * NODES * F_IN + NODES * F_OUT
 
 
 def sums_on_tensor(g):
-    return (3 * g + 5) % 8 < 3
+    return (3 * g + 3) % 8 < 3
 
 
 def tile_graphconvlayer_k_kernel(tc, X, W_gcn, b, H, Wd, out):
@@ -43,6 +44,7 @@ def tile_graphconvlayer_k_kernel(tc, X, W_gcn, b, H, Wd, out):
         loads = ctx.enter_context(tc.tile_pool(name="loads", bufs=LOADS_AHEAD + 2))
         work = ctx.enter_context(tc.tile_pool(name="work", bufs=2))
         regrouped = ctx.enter_context(tc.tile_pool(name="regrouped", bufs=3))
+        pairs = ctx.enter_context(tc.tile_pool(name="pairs", bufs=3))
         quant = ctx.enter_context(tc.tile_pool(name="quant", bufs=3))
         acc_pool = ctx.enter_context(tc.psum_pool(name="acc", bufs=1))
         xt_pool = ctx.enter_context(tc.psum_pool(name="xt", bufs=4))
@@ -81,7 +83,6 @@ def tile_graphconvlayer_k_kernel(tc, X, W_gcn, b, H, Wd, out):
 
         x_pass = {}
         x_middle = {}
-        xt_banks = {}
         w_pass = {}
         pair_sums = {}
         ax_grouped = {}
@@ -112,21 +113,20 @@ def tile_graphconvlayer_k_kernel(tc, X, W_gcn, b, H, Wd, out):
 
         def transpose_x(g):
             words = x_pass[g][:].bitcast(F32)
-            xt_banks[g] = []
             for bb in range(BATCH):
-                xt = xt_pool.tile([P, GRID * GRID, 2], F32, name="xt")
+                xt = xt_pool.tile([P, 2, GRID * GRID], F32, name="xt")
                 for u in range(2):
                     for half in range(2):
                         nc.tensor.transpose(
-                            xt[:, half * P : (half + 1) * P, u],
+                            xt[:, u, half * P : (half + 1) * P],
                             words[:, 2 * bb + half, u * P : (u + 1) * P],
                             ident[:],
                         )
+                inner = bordered[g % 3][:].bitcast(F32)[:, bb, 0:GRID, 2 : 2 + 2 * GRID]
                 nc.scalar.copy(
-                    out=bordered[g % 3][:].bitcast(F32)[:, bb, 0:GRID, 2 : 2 + 2 * GRID],
-                    in_=xt[:].rearrange("p (i j) u -> p i (j u)", j=GRID),
+                    out=inner.rearrange("p i (j u) -> p i j u", u=2),
+                    in_=xt[:].rearrange("p u (i j) -> p i j u", j=GRID),
                 )
-                xt_banks[g].append(xt)
 
         def sum_on_tensor(g):
             grouped = work.tile([P, NODES * PACK], BF16, name="ax_plain", align_bytes=64)
@@ -177,29 +177,35 @@ def tile_graphconvlayer_k_kernel(tc, X, W_gcn, b, H, Wd, out):
             w_codes[g] = codes
             w_scales[g] = scales
 
+        def copy_single_terms(g):
+            src = bordered[g % 3]
+            inner = GRID * PACK
+            pair = pairs.tile([P, BATCH, SUMS, PAIR_PITCH], F32, name="pair")
+            nc.scalar.copy(out=pair[:, :, 0, 0 : SUMS * PACK], in_=src[:, :, 0, :])
+            nc.scalar.copy(
+                out=pair[:, :, 1:SUMS, inner : inner + PACK], in_=src[:, :, 1:SUMS, inner : inner + PACK]
+            )
+            pair_sums[g] = pair
+
         def add_pairs(g):
             src = bordered[g % 3]
             inner = GRID * PACK
-            pair = work.tile([P, BATCH, SUMS, SUMS * PACK], F32, name="pair")
-            nc.vector.tensor_copy(out=pair[:, :, 0, :], in_=src[:, :, 0, :])
-            nc.vector.tensor_copy(out=pair[:, :, 1:SUMS, inner:], in_=src[:, :, 1:SUMS, inner:])
-            for bb in range(BATCH):
-                above = xt_banks[g][bb][:].bitcast(BF16).rearrange("p (i j) t -> p i (j t)", j=GRID)
-                nc.vector.tensor_tensor(
-                    out=pair[:, bb, 1:SUMS, 0:inner], in0=above, in1=src[:, bb, 1:SUMS, 0:inner], op=ADD
-                )
-            pair_sums[g] = pair
+            nc.vector.tensor_tensor(
+                out=pair_sums[g][:, :, 1:SUMS, 0:inner],
+                in0=src[:, :, 0:GRID, PACK : PACK + inner],
+                in1=src[:, :, 1:SUMS, 0:inner],
+                op=ADD,
+            )
 
         def add_sums(g):
             pair = pair_sums[g]
             grouped = work.tile([P, BATCH, GRID, GRID * PACK], BF16, name="ax_grouped", align_bytes=64)
-            for bb in range(BATCH):
-                nc.vector.tensor_tensor(
-                    out=grouped[:, bb],
-                    in0=pair[:, bb, 0:GRID, 0 : GRID * PACK],
-                    in1=pair[:, bb, 1 : 1 + GRID, PACK : PACK + GRID * PACK],
-                    op=ADD,
-                )
+            nc.vector.tensor_tensor(
+                out=grouped[:],
+                in0=pair[:, :, 0:GRID, 0 : GRID * PACK],
+                in1=pair[:, :, 1 : 1 + GRID, PACK : PACK + GRID * PACK],
+                op=ADD,
+            )
             ax_grouped[g] = grouped[:].rearrange("p b i c -> p (b i c)")
 
         def quantise_ax(g):
@@ -235,6 +241,7 @@ def tile_graphconvlayer_k_kernel(tc, X, W_gcn, b, H, Wd, out):
             else:
                 transpose_x(g)
                 regroup_w(g)
+                copy_single_terms(g)
 
         with tc.manual_schedule():
             for g in range(LOADS_AHEAD):
@@ -245,13 +252,13 @@ def tile_graphconvlayer_k_kernel(tc, X, W_gcn, b, H, Wd, out):
             prepare(1)
             nc.sync.dma_start(out=bias[:], in_=b.partition_broadcast(P))
             for g in range(PASSES):
+                if g + 2 < PASSES:
+                    prepare(g + 2)
                 if not sums_on_tensor(g):
                     add_sums(g)
                 if g >= 1:
                     quantise_ax(g - 1)
                     multiply(g - 1)
-                if g + 2 < PASSES:
-                    prepare(g + 2)
                 if g + 1 < PASSES:
                     if not sums_on_tensor(g + 1):
                         add_pairs(g + 1)

from contextlib import ExitStack

import concourse.masks as masks
import concourse.mybir as mybir

BF16 = mybir.dt.bfloat16
F32 = mybir.dt.float32
U32 = mybir.dt.uint32
U8 = mybir.dt.uint8
FP8X4 = mybir.dt.float8_e4m3fn_x4
ADD = mybir.AluOpType.add

P = 128
PACK = 4
K_PASS = P * PACK
BATCH = 2
GRID = 16
NODES = BATCH * GRID * GRID
F_IN = 16384
F_OUT = 512
PASSES = F_IN // K_PASS
NODE_TILES = NODES // P
LOADS_AHEAD = 6
SUMS = GRID + 1
PAIR_PITCH = (SUMS + 1) * PACK
MID_FIRST = 64

FLOPS = 2 * NODES * F_IN * F_OUT + 3 * NODES * F_IN + NODES * F_OUT


def sums_on_tensor(g):
    return (3 * g + 3) % 8 < 3


def tile_graphconvlayer_k_kernel(tc, X, W_gcn, b, H, Wd, out):
    nc = tc.nc
    assert H == GRID and Wd == GRID

    x_rows = X.rearrange("b n f -> (b n) f").rearrange("(r p) f -> p r f", p=P)
    out_rows = out.rearrange("b n o -> (b n) o")

    with ExitStack() as ctx:
        const = ctx.enter_context(tc.tile_pool(name="const", bufs=1))
        loads = ctx.enter_context(tc.tile_pool(name="loads", bufs=LOADS_AHEAD + 2))
        work = ctx.enter_context(tc.tile_pool(name="work", bufs=2))
        regrouped = ctx.enter_context(tc.tile_pool(name="regrouped", bufs=3))
        pairs = ctx.enter_context(tc.tile_pool(name="pairs", bufs=3))
        quant = ctx.enter_context(tc.tile_pool(name="quant", bufs=3))
        acc_pool = ctx.enter_context(tc.psum_pool(name="acc", bufs=1))
        xt_pool = ctx.enter_context(tc.psum_pool(name="xt", bufs=4))

        ident = const.tile([P, P], F32, name="ident")
        masks.make_identity(nc, ident[:])

        bordered = [
            const.tile([P, BATCH, SUMS, SUMS * PACK], BF16, name="bordered%d" % s) for s in range(3)
        ]
        for s in range(3):
            nc.vector.memset(bordered[s][:], 0.0)

        wide = const.tile([P, P + 2 * GRID], BF16, name="wide")
        nc.vector.memset(wide[:], 0.0)
        nc.vector.tensor_copy(out=wide[:, GRID : GRID + P], in_=ident[:])
        adjacency = const.tile([P, P], BF16, name="adjacency")
        nc.vector.tensor_tensor(
            out=adjacency[:], in0=wide[:, 0:P], in1=wide[:, 2 * GRID : 2 * GRID + P], op=ADD
        )
        by_row = adjacency[:].rearrange("p (i j) -> p i j", j=GRID)
        from_left = wide[:, GRID - 1 : GRID - 1 + P].rearrange("p (i j) -> p i j", j=GRID)
        from_right = wide[:, GRID + 1 : GRID + 1 + P].rearrange("p (i j) -> p i j", j=GRID)
        nc.vector.tensor_tensor(
            out=by_row[:, :, 1:GRID], in0=by_row[:, :, 1:GRID], in1=from_left[:, :, 1:GRID], op=ADD
        )
        nc.vector.tensor_tensor(
            out=by_row[:, :, 0 : GRID - 1],
            in0=by_row[:, :, 0 : GRID - 1],
            in1=from_right[:, :, 0 : GRID - 1],
            op=ADD,
        )

        acc = [acc_pool.tile([P, F_OUT], F32, name="acc%d" % r) for r in range(NODE_TILES)]
        bias = const.tile([P, F_OUT], BF16, name="bias")

        x_pass = {}
        x_middle = {}
        w_pass = {}
        pair_sums = {}
        ax_grouped = {}
        ax_codes = {}
        ax_scales = {}
        w_grouped = {}
        w_codes = {}
        w_scales = {}

        def load(g):
            features = slice(g * K_PASS, (g + 1) * K_PASS)
            x_sb = loads.tile([P, NODE_TILES, K_PASS], BF16, name="x_sb")
            nc.sync.dma_start(out=x_sb[:], in_=x_rows[:, :, features])
            x_pass[g] = x_sb
            if sums_on_tensor(g):
                x_mid = loads.tile([P, BATCH, K_PASS], BF16, name="x_mid")
                nc.sync.dma_start(
                    out=x_mid[:],
                    in_=X[:, MID_FIRST : MID_FIRST + P, features].rearrange("b p f -> p b f"),
                )
                x_middle[g] = x_mid
            w_sb = loads.tile([P, 2, 2 * F_OUT], BF16, name="w_sb")
            nc.sync.dma_start(
                out=w_sb[:],
                in_=W_gcn[features, :].rearrange("(u p e) o -> p u (e o)", p=P, e=2),
            )
            w_pass[g] = w_sb

        def transpose_x(g):
            words = x_pass[g][:].bitcast(F32)
            for bb in range(BATCH):
                xt = xt_pool.tile([P, 2, GRID * GRID], F32, name="xt")
                for u in range(2):
                    for half in range(2):
                        nc.tensor.transpose(
                            xt[:, u, half * P : (half + 1) * P],
                            words[:, 2 * bb + half, u * P : (u + 1) * P],
                            ident[:],
                        )
                inner = bordered[g % 3][:].bitcast(F32)[:, bb, 0:GRID, 2 : 2 + 2 * GRID]
                nc.scalar.copy(
                    out=inner.rearrange("p i (j u) -> p i j u", u=2),
                    in_=xt[:].rearrange("p u (i j) -> p i j u", j=GRID),
                )

        def sum_on_tensor(g):
            grouped = work.tile([P, NODES * PACK], BF16, name="ax_plain", align_bytes=64)
            edge = P - GRID
            for bb in range(BATCH):
                upper = xt_pool.tile([P, PACK, P], F32, name="xt")
                lower = xt_pool.tile([P, PACK, P], F32, name="xt")
                for t in range(PACK):
                    first = (t // 2) * (K_PASS // 2) + t % 2
                    last = (t // 2 + 1) * (K_PASS // 2)
                    x_up = x_pass[g][:, 2 * bb, first:last:2]
                    x_mid = x_middle[g][:, bb, first:last:2]
                    x_low = x_pass[g][:, 2 * bb + 1, first:last:2]
                    for dst, lhsT, columns in (
                        (upper[:, t, 0:edge], x_up, adjacency[:, 0:edge]),
                        (upper[:, t, edge:P], x_mid, adjacency[:, 3 * GRID : 4 * GRID]),
                        (lower[:, t, 0:GRID], x_mid, adjacency[:, 4 * GRID : 5 * GRID]),
                        (lower[:, t, GRID:P], x_low, adjacency[:, GRID:P]),
                    ):
                        nc.tensor.matmul(out=dst, lhsT=lhsT, rhs=columns, start=True, stop=True)
                for half, bank in enumerate((upper, lower)):
                    r = 2 * bb + half
                    nc.scalar.copy(
                        out=grouped[:, r * P * PACK : (r + 1) * P * PACK].rearrange(
                            "p (n t) -> p n t", t=PACK
                        ),
                        in_=bank[:].rearrange("p t n -> p n t"),
                    )
            ax_grouped[g] = grouped[:]

        def regroup_w(g):
            rows = w_pass[g][:].rearrange("p u (e o) -> p (u e) o", e=2)
            grouped = regrouped.tile([P, F_OUT, PACK], BF16, name="w_grouped", align_bytes=64)
            nc.scalar.copy(
                out=grouped[:].rearrange("p (c i) t -> p c t i", i=4),
                in_=rows.rearrange("p t (c i) -> p c t i", i=4),
            )
            w_grouped[g] = grouped

        def quantise_w(g):
            codes = quant.tile([P, F_OUT], U32, name="w_codes", align_bytes=64)
            scales = quant.tile([P, F_OUT], U8, name="w_scales", align_bytes=64)
            nc.vector.quantize_mx(
                out=codes[:].bitcast(FP8X4),
                scales=scales[:],
                in_=w_grouped[g][:].rearrange("p o t -> p (o t)"),
            )
            w_codes[g] = codes
            w_scales[g] = scales

        def copy_single_terms(g):
            src = bordered[g % 3]
            inner = GRID * PACK
            pair = pairs.tile([P, BATCH, SUMS, PAIR_PITCH], F32, name="pair")
            nc.scalar.copy(out=pair[:, :, 0, 0 : SUMS * PACK], in_=src[:, :, 0, :])
            nc.scalar.copy(
                out=pair[:, :, 1:SUMS, inner : inner + PACK], in_=src[:, :, 1:SUMS, inner : inner + PACK]
            )
            pair_sums[g] = pair

        def add_pairs(g):
            src = bordered[g % 3]
            inner = GRID * PACK
            nc.vector.tensor_tensor(
                out=pair_sums[g][:, :, 1:SUMS, 0:inner],
                in0=src[:, :, 0:GRID, PACK : PACK + inner],
                in1=src[:, :, 1:SUMS, 0:inner],
                op=ADD,
            )

        def add_sums(g):
            pair = pair_sums[g]
            grouped = work.tile([P, BATCH, GRID, GRID * PACK], BF16, name="ax_grouped", align_bytes=64)
            nc.vector.tensor_tensor(
                out=grouped[:],
                in0=pair[:, :, 0:GRID, 0 : GRID * PACK],
                in1=pair[:, :, 1 : 1 + GRID, PACK : PACK + GRID * PACK],
                op=ADD,
            )
            ax_grouped[g] = grouped[:].rearrange("p b i c -> p (b i c)")

        def quantise_ax(g):
            codes = quant.tile([P, NODES], U32, name="ax_codes", align_bytes=64)
            scales = quant.tile([P, NODES], U8, name="ax_scales", align_bytes=64)
            nc.vector.quantize_mx(
                out=codes[:].bitcast(FP8X4),
                scales=scales[:],
                in_=ax_grouped[g],
            )
            ax_codes[g] = codes
            ax_scales[g] = scales

        def multiply(g):
            for r in range(NODE_TILES):
                nodes = slice(r * P, (r + 1) * P)
                nc.tensor.matmul_mx(
                    out=acc[r][:],
                    lhsT=ax_codes[g][:, nodes].bitcast(FP8X4),
                    lhsT_scale=ax_scales[g][:, nodes],
                    rhs=w_codes[g][:].bitcast(FP8X4),
                    rhs_scale=w_scales[g][:],
                    start=(g == 0),
                    stop=(g == PASSES - 1),
                )

        def prepare(g):
            if g + LOADS_AHEAD < PASSES:
                load(g + LOADS_AHEAD)
            if sums_on_tensor(g):
                regroup_w(g)
                sum_on_tensor(g)
            else:
                transpose_x(g)
                regroup_w(g)
                copy_single_terms(g)

        with tc.manual_schedule():
            for g in range(LOADS_AHEAD):
                load(g)
            prepare(0)
            add_pairs(0)
            quantise_w(0)
            prepare(1)
            nc.sync.dma_start(out=bias[:], in_=b.partition_broadcast(P))
            for g in range(PASSES):
                if g + 2 < PASSES:
                    prepare(g + 2)
                if not sums_on_tensor(g):
                    add_sums(g)
                if g >= 1:
                    quantise_ax(g - 1)
                    multiply(g - 1)
                if g + 1 < PASSES:
                    if not sums_on_tensor(g + 1):
                        add_pairs(g + 1)
                    quantise_w(g + 1)
            quantise_ax(PASSES - 1)
            multiply(PASSES - 1)

            for r in range(NODE_TILES):
                result = work.tile([P, F_OUT], F32, name="result")
                nc.vector.tensor_tensor(out=result[:], in0=acc[r][:], in1=bias[:], op=ADD)
                nc.sync.dma_start(out=out_rows[r * P : (r + 1) * P, :], in_=result[:])
